import numpy as np
import ml_dtypes


def mxq(x, axis, fmt="e4m3"):
    dtype, down = {"e4m3": (ml_dtypes.float8_e4m3fn, 7), "e5m2": (ml_dtypes.float8_e5m2, 14)}[fmt]
    v = np.moveaxis(np.asarray(x, np.float32).astype(ml_dtypes.bfloat16).astype(np.float64), axis, -1)
    blocks = v.reshape(v.shape[:-1] + (-1, 32))
    amax = np.abs(blocks).max(-1, keepdims=True)
    byte = np.maximum(np.where(amax > 0, np.frexp(amax)[1] - 1 + 127, 0) - down, 1)
    scale = np.exp2(byte - 127.0)
    codes = (blocks / scale).astype(np.float32).astype(dtype).astype(np.float64)
    return np.moveaxis((codes * scale).reshape(v.shape), -1, axis)


WIDE = False


def mx_kscale(k):
    if not WIDE:
        return np.ones(k)
    levels = np.array([10, -10, 5, -5, 0])
    if k % 512:
        return np.exp2(np.random.permutation(np.resize(levels, k // 32))).repeat(32)
    a = np.empty((k // 512, 16))
    for p in range(k // 512):
        a[p, :8] = np.random.permutation(np.resize(levels, 8))
        for g in range(8):
            far = levels[np.abs(levels - a[p, g]) >= 10]
            a[p, g + 8] = far[np.random.randint(len(far))]
    return np.exp2(a.ravel()).repeat(32)


BF16 = ml_dtypes.bfloat16


def bf(x):
    return np.asarray(x, np.float32).astype(BF16)


def f64(x):
    return np.asarray(x).astype(np.float64)


B, SI, ST, DM, H, D = 4, 1536, 512, 1024, 1, 128
S = ST + SI
HD = H * D
EPS = 1e-6


def rms_norm(x, gamma):
    var = np.mean(x * x, axis=-1, keepdims=True)
    return x * (1.0 / np.sqrt(var + EPS)) * gamma


def apply_rotary(x, cos, sin):
    xr = x.reshape(B, S, H, D // 2, 2)
    x1, x2 = xr[..., 0], xr[..., 1]
    rot = np.stack([-x2, x1], axis=-1).reshape(B, S, H, D)
    return x * cos[None, :, None, :] + rot * sin[None, :, None, :]


def heads(y):
    return y.reshape(B, -1, H, D)


def setup_inputs():
    s = mx_kscale(DM)
    w = 1.0 / np.sqrt(DM)
    pos = np.arange(S)[:, None]
    inv = 1.0 / (10000.0 ** (np.arange(0, D, 2) / D))
    ang = np.repeat(pos * inv[None, :], 2, axis=-1)
    inp = {"hidden_states": bf(np.random.standard_normal((B, SI, DM)) * s),
           "encoder_hidden_states": bf(np.random.standard_normal((B, ST, DM)) * s),
           "rope_cos": bf(np.cos(ang)), "rope_sin": bf(np.sin(ang))}
    for n in ["Wq", "Wk", "Waq", "Wak"]:
        inp[n] = bf(np.random.standard_normal((DM, HD)) * w / s[:, None])
    for n in ["bq", "bk", "baq", "bak"]:
        inp[n] = bf(np.random.standard_normal(HD) * 0.3)
    for n in ["g_q", "g_k", "g_aq", "g_ak"]:
        inp[n] = bf(1.5 * (1.0 + 0.1 * np.random.standard_normal(D)))
    return inp


def reference(hidden_states, encoder_hidden_states, rope_cos, rope_sin, Wq, bq, Wk, bk, Waq, baq, Wak, bak, g_q, g_k, g_aq, g_ak):
    xq = mxq(f64(hidden_states), 2, "e4m3")
    cq = mxq(f64(encoder_hidden_states), 2, "e4m3")
    q = rms_norm(heads((xq @ mxq(f64(Wq), 0, "e4m3")) + f64(bq)), f64(g_q))
    k = rms_norm(heads((xq @ mxq(f64(Wk), 0, "e4m3")) + f64(bk)), f64(g_k))
    eq = rms_norm(heads((cq @ mxq(f64(Waq), 0, "e4m3")) + f64(baq)), f64(g_aq))
    ek = rms_norm(heads((cq @ mxq(f64(Wak), 0, "e4m3")) + f64(bak)), f64(g_ak))
    q = np.concatenate([eq, q], axis=1)
    k = np.concatenate([ek, k], axis=1)
    return apply_rotary(q, f64(rope_cos), f64(rope_sin)), apply_rotary(k, f64(rope_cos), f64(rope_sin))

@@ -1,0 +1,305 @@
+from contextlib import ExitStack
+
+import concourse.mybir as mybir
+from concourse.masks import make_identity
+
+F32 = mybir.dt.float32
+BF16 = mybir.dt.bfloat16
+U32 = mybir.dt.uint32
+U8 = mybir.dt.uint8
+FP8X4 = mybir.dt.float8_e4m3fn_x4
+ACT = mybir.ActivationFunctionType
+ALU = mybir.AluOpType
+
+P = 128
+BATCH = 4
+K = 1024
+D = 128
+HALF = D // 2
+EPS = 1e-6
+BLOCK = 512
+T = BLOCK // P
+BLOCKS = 4
+GROUPS = BLOCKS * BATCH
+PASSES = K // 512
+WORD_TILES = K // 2 // P
+LOOKAHEAD = 4
+
+FLOPS = 2 * BATCH * BLOCKS * BLOCK * K * 2 * D
+
+
+def tile_fluxjointattention_pa_t_kernel(
+    tc,
+    hidden_states,
+    encoder_hidden_states,
+    rope_cos,
+    rope_sin,
+    Wq,
+    Wk,
+    Waq,
+    Wak,
+    bq,
+    bk,
+    baq,
+    bak,
+    g_q,
+    g_k,
+    g_aq,
+    g_ak,
+    out_0,
+    out_1,
+):
+    nc = tc.nc
+    outs = (out_0, out_1)
+    weights = (Waq, Wak, Wq, Wk)
+    biases = (baq, bak, bq, bk)
+    gains = (g_aq, g_ak, g_q, g_k)
+
+    with ExitStack() as ctx:
+        consts = ctx.enter_context(tc.tile_pool(name="consts", bufs=1))
+        work = ctx.enter_context(tc.tile_pool(name="work", bufs=2))
+        psum = ctx.enter_context(tc.psum_pool(name="psum", bufs=1))
+
+        x_tiles = {}
+        grouped_tiles = {}
+        mx_tiles = {}
+        yt_tiles = {}
+        ybt_tiles = {}
+        ybp_tiles = {}
+        r_tiles = {}
+
+        def load_x(g):
+            block, b = divmod(g, BATCH)
+            if block == 0:
+                rows = encoder_hidden_states[b]
+            else:
+                rows = hidden_states[b, (block - 1) * BLOCK : block * BLOCK, :]
+            x_sb = work.tile([P, T * K], BF16, tag="x", bufs=LOOKAHEAD + 2)
+            nc.sync.dma_start(out=x_sb[:], in_=rows.rearrange("(p t) k -> p (t k)", t=T))
+            x_tiles[g] = x_sb
+
+        warm = consts.tile([P, 1], F32)
+        nc.vector.memset(warm[:], 1.0)
+        nc.scalar.activation(out=warm[:], in_=warm[:], func=ACT.Sqrt)
+
+        bias_rows = consts.tile([P, P], BF16)
+        nc.vector.memset(bias_rows[:], 0.0)
+        gain_rows = consts.tile([P, 4 * D], BF16)
+        nc.vector.memset(gain_rows[:], 0.0)
+        ones = consts.tile([P, P], BF16)
+        nc.vector.memset(ones[:], 1.0)
+
+        ident = consts.tile([P, P], F32)
+        make_identity(nc, ident[:])
+        ident_bf = consts.tile([P, P], BF16)
+        nc.vector.tensor_copy(out=ident_bf[:], in_=ident[:])
+
+        w_raw = {}
+
+        def load_weights(stream):
+            raw = consts.tile([P, 2 * K * D // P], BF16, name="w_raw%d" % stream)
+            for qk in range(2):
+                nc.sync.dma_start(
+                    out=raw[:, qk * 1024 : (qk + 1) * 1024].rearrange("p (c f) -> p c f", c=PASSES),
+                    in_=weights[2 * stream + qk].rearrange("(c p j) n -> p c (j n)", c=PASSES, p=P, j=4),
+                )
+            w_raw[stream] = raw
+
+        load_x(0)
+        load_weights(0)
+        for j in range(4):
+            nc.sync.dma_start(out=bias_rows[j : j + 1, :], in_=biases[j].unsqueeze(0))
+            nc.sync.dma_start(out=gain_rows[0:1, j * D : (j + 1) * D], in_=gains[j].unsqueeze(0))
+        load_x(1)
+        cos_sb = consts.tile([P, BLOCKS, T * D], BF16)
+        nc.sync.dma_start(out=cos_sb[:], in_=rope_cos.rearrange("(c p t) d -> p c (t d)", c=BLOCKS, p=P, t=T))
+        sin_sb = consts.tile([P, BLOCKS, T * D], BF16)
+        nc.sync.dma_start(out=sin_sb[:], in_=rope_sin.rearrange("(c p t) d -> p c (t d)", c=BLOCKS, p=P, t=T))
+        load_x(2)
+        load_x(3)
+        load_weights(1)
+
+        w_codes = {}
+        w_scales = {}
+
+        def quantise_weights(stream):
+            grouped = consts.tile([P, 2048], BF16, name="w_grouped%d" % stream, align_bytes=64)
+            nc.vector.tensor_copy(
+                out=grouped[:].rearrange("p (m n j) -> p m n j", m=4, j=4),
+                in_=w_raw[stream][:].rearrange("p (m j n) -> p m n j", m=4, j=4),
+            )
+            codes = consts.tile([P, 512], U32, name="w_codes%d" % stream, align_bytes=64)
+            scales = consts.tile([P, 512], U8, name="w_scales%d" % stream, align_bytes=64)
+            nc.vector.quantize_mx(out=codes[:].bitcast(FP8X4), scales=scales[:], in_=grouped[:])
+            w_codes[stream] = codes
+            w_scales[stream] = scales
+
+        bias_col = consts.tile([P, 4], F32)
+        gain_pairs = consts.tile([P, 4, 3, HALF], F32)
+
+        def spread_vectors():
+            bias_ps = psum.tile([P, P], BF16, tag="ybp", bufs=2)
+            nc.tensor.transpose(bias_ps[:], bias_rows[:], ident_bf[:])
+            nc.vector.tensor_copy(out=bias_col[:], in_=bias_ps[:, 0:4])
+            gain_ps = psum.tile([P, 4 * D], F32, tag="yt", bufs=2)
+            nc.tensor.matmul(out=gain_ps[:], lhsT=ones[:], rhs=gain_rows[:], start=True, stop=True)
+            nc.vector.tensor_copy(
+                out=gain_pairs[:, :, 0:2, :], in_=gain_ps[:].rearrange("p (j i h) -> p j h i", j=4, h=2)
+            )
+            nc.vector.tensor_scalar_mul(out=gain_pairs[:, :, 2, :], in0=gain_pairs[:, :, 1, :], scalar1=-1.0)
+
+        even_tabs = {}
+        odd_tabs = {}
+
+        def build_tables(block, qk):
+            j = 2 * min(block, 1) + qk
+            cos_pairs = cos_sb[:, block, :].rearrange("p (t i h) -> p t h i", t=T, h=2)
+            sin_pairs = sin_sb[:, block, :].rearrange("p (t i h) -> p t h i", t=T, h=2)
+            even_tab = consts.tile([P, T, 2, HALF], F32, name="even_tab%d_%d" % (block, qk))
+            odd_tab = consts.tile([P, T, 2, HALF], F32, name="odd_tab%d_%d" % (block, qk))
+            for table, h, angles, gain in (
+                (even_tab, 0, cos_pairs, 0),
+                (even_tab, 1, sin_pairs, 0),
+                (odd_tab, 0, sin_pairs, 2),
+                (odd_tab, 1, cos_pairs, 1),
+            ):
+                nc.gpsimd.tensor_tensor(
+                    out=table[:, :, h, :],
+                    in0=angles[:, :, h, :],
+                    in1=gain_pairs[:, j, gain, :].unsqueeze(1).to_broadcast([P, T, HALF]),
+                    op=ALU.mult,
+                )
+            even_tabs[(block, qk)] = even_tab
+            odd_tabs[(block, qk)] = odd_tab
+
+        def transpose_x(g):
+            x_words = x_tiles[g][:].bitcast(F32)
+            grouped = work.tile([P, PASSES * BLOCK * 4], BF16, tag="grouped", bufs=2, align_bytes=64)
+            grouped_words = grouped[:].bitcast(F32).rearrange("p (c n u) -> p c n u", c=PASSES, u=2)
+            for t in range(T):
+                xt = psum.tile([P, WORD_TILES, P], F32, tag="xt", bufs=4)
+                for a in range(WORD_TILES):
+                    c, u = divmod(a, 2)
+                    first = t * (K // 2) + c * 2 * P
+                    nc.tensor.transpose(xt[:, a, :], x_words[:, first + u : first + 2 * P : 2], ident[:])
+                copy_out = nc.vector.tensor_copy if t == T - 1 else nc.scalar.copy
+                copy_out(
+                    out=grouped_words[:, :, t * P : (t + 1) * P, :],
+                    in_=xt[:].rearrange("p (c u) n -> p c n u", c=PASSES),
+                )
+            grouped_tiles[g] = grouped
+
+        def quantise_x(g):
+            grouped = grouped_tiles[g]
+            codes = work.tile([P, PASSES * BLOCK], U32, tag="codes", bufs=2, align_bytes=64)
+            scales = work.tile([P, PASSES * BLOCK], U8, tag="scales", bufs=2, align_bytes=64)
+            nc.vector.quantize_mx(out=codes[:].bitcast(FP8X4), scales=scales[:], in_=grouped[:])
+            mx_tiles[g] = (codes, scales)
+
+        def project(g):
+            stream = min(g // BATCH, 1)
+            codes, scales = mx_tiles[g]
+            for qk in range(2):
+                yt = psum.tile([P, BLOCK], F32, tag="yt", bufs=2)
+                for c in range(PASSES):
+                    w_cols = slice((2 * qk + c) * P, (2 * qk + c + 1) * P)
+                    x_cols = slice(c * BLOCK, (c + 1) * BLOCK)
+                    nc.tensor.matmul_mx(
+                        out=yt[:],
+                        lhsT=w_codes[stream][:, w_cols].bitcast(FP8X4),
+                        lhsT_scale=w_scales[stream][:, w_cols],
+                        rhs=codes[:, x_cols].bitcast(FP8X4),
+                        rhs_scale=scales[:, x_cols],
+                        start=(c == 0),
+                        stop=(c == PASSES - 1),
+                    )
+                yt_tiles[(g, qk)] = yt
+
+        def add_bias(g):
+            stream = min(g // BATCH, 1)
+            for qk in range(2):
+                ybt = work.tile([P, BLOCK], F32, tag="ybt", bufs=4)
+                j = 2 * stream + qk
+                nc.scalar.activation(
+                    out=ybt[:], in_=yt_tiles[(g, qk)][:], func=ACT.Identity, bias=bias_col[:, j : j + 1]
+                )
+                ybt_tiles[(g, qk)] = ybt
+
+        def transpose_back(g):
+            for qk in range(2):
+                ybt = ybt_tiles[(g, qk)]
+                ybp = psum.tile([P, T, D], F32, tag="ybp", bufs=2)
+                for t in range(T):
+                    nc.tensor.transpose(ybp[:, t, :], ybt[:, t * P : (t + 1) * P], ident[:])
+                ybp_tiles[(g, qk)] = ybp
+
+        def norms(g):
+            ss = work.tile([P, 2 * T], F32, tag="ss", bufs=3)
+            for qk in range(2):
+                for t in range(T):
+                    squares = work.tile([P, D], F32, tag="squares", bufs=2)
+                    nc.scalar.activation(
+                        out=squares[:],
+                        in_=ybp_tiles[(g, qk)][:, t, :],
+                        func=ACT.Square,
+                        accum_out=ss[:, qk * T + t : qk * T + t + 1],
+                    )
+            rms = work.tile([P, 2 * T], F32, tag="rms", bufs=3)
+            nc.scalar.activation(out=rms[:], in_=ss[:], func=ACT.Sqrt, scale=1.0 / D, bias=EPS)
+            r = work.tile([P, 2 * T], F32, tag="r", bufs=3)
+            nc.vector.reciprocal(out=r[:], in_=rms[:])
+            r_tiles[g] = r
+
+        def rotate_and_store(g):
+            block, b = divmod(g, BATCH)
+            r = r_tiles[g]
+            for qk in range(2):
+                ybp = ybp_tiles[(g, qk)]
+                from_even = work.tile([P, T, D], F32, tag="from_even", bufs=4)
+                from_odd = work.tile([P, T, D], F32, tag="from_odd", bufs=4)
+                for t in range(T):
+                    col = qk * T + t
+                    pairs = ybp[:, t, :].rearrange("p (i h) -> p i h", h=2)
+                    for h, tabs, part in ((0, even_tabs, from_even), (1, odd_tabs, from_odd)):
+                        nc.vector.scalar_tensor_tensor(
+                            out=part[:, t, :].rearrange("p (i h) -> p i h", h=2),
+                            in0=pairs[:, :, h : h + 1].to_broadcast([P, HALF, 2]),
+                            scalar=r[:, col : col + 1],
+                            in1=tabs[(block, qk)][:, t, :, :].rearrange("p h i -> p i h"),
+                            op0=ALU.mult,
+                            op1=ALU.mult,
+                        )
+                result = work.tile([P, T, D], F32, tag="result", bufs=4)
+                nc.gpsimd.tensor_tensor(out=result[:], in0=from_even[:], in1=from_odd[:], op=ALU.add)
+                nc.sync.dma_start(
+                    out=outs[qk][b, block * BLOCK : (block + 1) * BLOCK, 0, :].rearrange("(p t) d -> p t d", t=T),
+                    in_=result[:],
+                )
+
+        with tc.manual_schedule():
+            for i in range(GROUPS + 3):
+                if i + LOOKAHEAD < GROUPS:
+                    load_x(i + LOOKAHEAD)
+                if 0 <= i - 3 < GROUPS:
+                    rotate_and_store(i - 3)
+                if 0 <= i - 2 < GROUPS:
+                    add_bias(i - 2)
+                if i < GROUPS:
+                    transpose_x(i)
+                if i == 0:
+                    spread_vectors()
+                    quantise_weights(0)
+                    for qk in range(2):
+                        build_tables(0, qk)
+                if i == 3:
+                    quantise_weights(1)
+                if i % BATCH < 2 and i // BATCH + 1 < BLOCKS:
+                    build_tables(i // BATCH + 1, i % BATCH)
+                if 0 <= i - 2 < GROUPS:
+                    transpose_back(i - 2)
+                if 0 <= i - 1 < GROUPS:
+                    project(i - 1)
+                if i < GROUPS:
+                    quantise_x(i)
+                if 0 <= i - 2 < GROUPS:
+                    norms(i - 2)

@@ -21,9 +21,14 @@ BLOCK = 512
 T = BLOCK // P
 BLOCKS = 4
 GROUPS = BLOCKS * BATCH
+UT = 2
+UNIT = UT * P
+UNITS_PER_GROUP = T // UT
+UNITS = GROUPS * UNITS_PER_GROUP
+UNITS_PER_BLOCK = UNITS // BLOCKS
 PASSES = K // 512
 WORD_TILES = K // 2 // P
-LOOKAHEAD = 4
+LOOKAHEAD = 5
 
 FLOPS = 2 * BATCH * BLOCKS * BLOCK * K * 2 * D
 
@@ -67,20 +72,32 @@ def tile_fluxjointattention_pa_t_kernel(
         ybt_tiles = {}
         ybp_tiles = {}
         r_tiles = {}
+        product_tiles = {}
+        result_tiles = {}
 
-        def load_x(g):
+        def load_x(g, pieces=1):
             block, b = divmod(g, BATCH)
             if block == 0:
                 rows = encoder_hidden_states[b]
             else:
                 rows = hidden_states[b, (block - 1) * BLOCK : block * BLOCK, :]
-            x_sb = work.tile([P, T * K], BF16, tag="x", bufs=LOOKAHEAD + 2)
-            nc.sync.dma_start(out=x_sb[:], in_=rows.rearrange("(p t) k -> p (t k)", t=T))
-            x_tiles[g] = x_sb
+            rows = rows.rearrange("(p t) k -> p (t k)", t=T)
+            if g not in x_tiles:
+                x_sb = work.tile([P, T * K], BF16, tag="x", bufs=LOOKAHEAD + 2)
+                x_tiles[g] = x_sb
+            return [
+                (x_tiles[g][:, c * T * K // pieces : (c + 1) * T * K // pieces],
+                 rows[:, c * T * K // pieces : (c + 1) * T * K // pieces])
+                for c in range(pieces)
+            ]
+
+        def fetch(pairs):
+            for dst, src in pairs:
+                nc.sync.dma_start(out=dst, in_=src)
 
         warm = consts.tile([P, 1], F32)
         nc.vector.memset(warm[:], 1.0)
-        nc.scalar.activation(out=warm[:], in_=warm[:], func=ACT.Sqrt)
+        nc.scalar.activation(out=warm[:], in_=warm[:], func=ACT.Abs_reciprocal_sqrt)
 
         bias_rows = consts.tile([P, P], BF16)
         nc.vector.memset(bias_rows[:], 0.0)
@@ -105,19 +122,23 @@ def tile_fluxjointattention_pa_t_kernel(
                 )
             w_raw[stream] = raw
 
-        load_x(0)
+        first_x = load_x(0, UNITS_PER_GROUP)
+        fetch(first_x[:1])
         load_weights(0)
+        fetch(first_x[1:])
         for j in range(4):
-            nc.sync.dma_start(out=bias_rows[j : j + 1, :], in_=biases[j].unsqueeze(0))
-            nc.sync.dma_start(out=gain_rows[0:1, j * D : (j + 1) * D], in_=gains[j].unsqueeze(0))
-        load_x(1)
+            nc.scalar.dma_start(out=bias_rows[j : j + 1, :], in_=biases[j].unsqueeze(0))
+        for j in range(4):
+            nc.scalar.dma_start(out=gain_rows[0:1, j * D : (j + 1) * D], in_=gains[j].unsqueeze(0))
+        fetch(load_x(1))
         cos_sb = consts.tile([P, BLOCKS, T * D], BF16)
         nc.sync.dma_start(out=cos_sb[:], in_=rope_cos.rearrange("(c p t) d -> p c (t d)", c=BLOCKS, p=P, t=T))
         sin_sb = consts.tile([P, BLOCKS, T * D], BF16)
         nc.sync.dma_start(out=sin_sb[:], in_=rope_sin.rearrange("(c p t) d -> p c (t d)", c=BLOCKS, p=P, t=T))
-        load_x(2)
-        load_x(3)
+        fetch(load_x(2))
+        fetch(load_x(3))
         load_weights(1)
+        fetch(load_x(4))
 
         w_codes = {}
         w_scales = {}
@@ -141,71 +162,85 @@ def tile_fluxjointattention_pa_t_kernel(
             bias_ps = psum.tile([P, P], BF16, tag="ybp", bufs=2)
             nc.tensor.transpose(bias_ps[:], bias_rows[:], ident_bf[:])
             nc.vector.tensor_copy(out=bias_col[:], in_=bias_ps[:, 0:4])
-            gain_ps = psum.tile([P, 4 * D], F32, tag="yt", bufs=2)
+            gain_ps = psum.tile([P, 4 * D], F32, tag="ybp", bufs=2)
             nc.tensor.matmul(out=gain_ps[:], lhsT=ones[:], rhs=gain_rows[:], start=True, stop=True)
             nc.vector.tensor_copy(
                 out=gain_pairs[:, :, 0:2, :], in_=gain_ps[:].rearrange("p (j i h) -> p j h i", j=4, h=2)
             )
             nc.vector.tensor_scalar_mul(out=gain_pairs[:, :, 2, :], in0=gain_pairs[:, :, 1, :], scalar1=-1.0)
 
-        even_tabs = {}
-        odd_tabs = {}
+        tables = {}
 
-        def build_tables(block, qk):
+        def table_steps(block, qk):
             j = 2 * min(block, 1) + qk
             cos_pairs = cos_sb[:, block, :].rearrange("p (t i h) -> p t h i", t=T, h=2)
             sin_pairs = sin_sb[:, block, :].rearrange("p (t i h) -> p t h i", t=T, h=2)
             even_tab = consts.tile([P, T, 2, HALF], F32, name="even_tab%d_%d" % (block, qk))
             odd_tab = consts.tile([P, T, 2, HALF], F32, name="odd_tab%d_%d" % (block, qk))
-            for table, h, angles, gain in (
-                (even_tab, 0, cos_pairs, 0),
-                (even_tab, 1, sin_pairs, 0),
-                (odd_tab, 0, sin_pairs, 2),
-                (odd_tab, 1, cos_pairs, 1),
-            ):
-                nc.gpsimd.tensor_tensor(
-                    out=table[:, :, h, :],
-                    in0=angles[:, :, h, :],
-                    in1=gain_pairs[:, j, gain, :].unsqueeze(1).to_broadcast([P, T, HALF]),
-                    op=ALU.mult,
+            tables[(block, qk, 0)] = even_tab
+            tables[(block, qk, 1)] = odd_tab
+            return [
+                (table, h, angles, gain_pairs[:, j, gain, :])
+                for table, h, angles, gain in (
+                    (even_tab, 0, cos_pairs, 0),
+                    (even_tab, 1, sin_pairs, 0),
+                    (odd_tab, 0, sin_pairs, 2),
+                    (odd_tab, 1, cos_pairs, 1),
                 )
-            even_tabs[(block, qk)] = even_tab
-            odd_tabs[(block, qk)] = odd_tab
+            ]
 
-        def transpose_x(g):
+        def build_table(step):
+            table, h, angles, gain = step
+            nc.gpsimd.tensor_tensor(
+                out=table[:, :, h, :],
+                in0=angles[:, :, h, :],
+                in1=gain.unsqueeze(1).to_broadcast([P, T, HALF]),
+                op=ALU.mult,
+            )
+
+        def place(u):
+            g, half = divmod(u, UNITS_PER_GROUP)
+            return g, half * UT, min(g // BATCH, 1)
+
+        def transpose_x(u):
+            g, t0, _ = place(u)
             x_words = x_tiles[g][:].bitcast(F32)
-            grouped = work.tile([P, PASSES * BLOCK * 4], BF16, tag="grouped", bufs=2, align_bytes=64)
-            grouped_words = grouped[:].bitcast(F32).rearrange("p (c n u) -> p c n u", c=PASSES, u=2)
-            for t in range(T):
+            banks = []
+            for tt in range(UT):
                 xt = psum.tile([P, WORD_TILES, P], F32, tag="xt", bufs=4)
                 for a in range(WORD_TILES):
-                    c, u = divmod(a, 2)
-                    first = t * (K // 2) + c * 2 * P
-                    nc.tensor.transpose(xt[:, a, :], x_words[:, first + u : first + 2 * P : 2], ident[:])
-                copy_out = nc.vector.tensor_copy if t == T - 1 else nc.scalar.copy
-                copy_out(
-                    out=grouped_words[:, :, t * P : (t + 1) * P, :],
-                    in_=xt[:].rearrange("p (c u) n -> p c n u", c=PASSES),
-                )
-            grouped_tiles[g] = grouped
+                    c, w = divmod(a, 2)
+                    first = (t0 + tt) * (K // 2) + c * 2 * P
+                    nc.tensor.transpose(xt[:, a, :], x_words[:, first + w : first + 2 * P : 2], ident[:])
+                banks.append(xt)
+            grouped = work.tile([P, PASSES * UNIT * 4], BF16, tag="grouped", bufs=3, align_bytes=64)
+            grouped_tiles[u] = (grouped, banks)
 
-        def quantise_x(g):
-            grouped = grouped_tiles[g]
-            codes = work.tile([P, PASSES * BLOCK], U32, tag="codes", bufs=2, align_bytes=64)
-            scales = work.tile([P, PASSES * BLOCK], U8, tag="scales", bufs=2, align_bytes=64)
+        def copy_x(u, tt, copy_out):
+            grouped, banks = grouped_tiles[u]
+            words = grouped[:].bitcast(F32).rearrange("p (c n w) -> p c n w", c=PASSES, w=2)
+            copy_out(
+                out=words[:, :, tt * P : (tt + 1) * P, :],
+                in_=banks[tt][:].rearrange("p (c w) n -> p c n w", c=PASSES),
+            )
+
+        def quantise_x(u):
+            grouped, _ = grouped_tiles[u]
+            codes = work.tile([P, PASSES * UNIT], U32, tag="codes", bufs=3, align_bytes=64)
+            scales = work.tile([P, PASSES * UNIT], U8, tag="scales", bufs=3, align_bytes=64)
             nc.vector.quantize_mx(out=codes[:].bitcast(FP8X4), scales=scales[:], in_=grouped[:])
-            mx_tiles[g] = (codes, scales)
+            mx_tiles[u] = (codes, scales)
 
-        def project(g):
-            stream = min(g // BATCH, 1)
-            codes, scales = mx_tiles[g]
+        def project(u):
+            _, _, stream = place(u)
+            codes, scales = mx_tiles[u]
+            yt = psum.tile([P, 2, UNIT], F32, tag="yt", bufs=2)
             for qk in range(2):
-                yt = psum.tile([P, BLOCK], F32, tag="yt", bufs=2)
                 for c in range(PASSES):
                     w_cols = slice((2 * qk + c) * P, (2 * qk + c + 1) * P)
-                    x_cols = slice(c * BLOCK, (c + 1) * BLOCK)
+                    x_cols = slice(c * UNIT, (c + 1) * UNIT)
                     nc.tensor.matmul_mx(
-                        out=yt[:],
+                        out=yt[:, qk, :],
                         lhsT=w_codes[stream][:, w_cols].bitcast(FP8X4),
                         lhsT_scale=w_scales[stream][:, w_cols],
                         rhs=codes[:, x_cols].bitcast(FP8X4),
@@ -213,93 +248,122 @@ def tile_fluxjointattention_pa_t_kernel(
                         start=(c == 0),
                         stop=(c == PASSES - 1),
                     )
-                yt_tiles[(g, qk)] = yt
+            yt_tiles[u] = yt
 
-        def add_bias(g):
-            stream = min(g // BATCH, 1)
+        def add_bias(u):
+            _, _, stream = place(u)
+            ybt = work.tile([P, 2, UNIT], F32, tag="ybt", bufs=3)
             for qk in range(2):
-                ybt = work.tile([P, BLOCK], F32, tag="ybt", bufs=4)
                 j = 2 * stream + qk
                 nc.scalar.activation(
-                    out=ybt[:], in_=yt_tiles[(g, qk)][:], func=ACT.Identity, bias=bias_col[:, j : j + 1]
+                    out=ybt[:, qk, :], in_=yt_tiles[u][:, qk, :], func=ACT.Identity, bias=bias_col[:, j : j + 1]
                 )
-                ybt_tiles[(g, qk)] = ybt
+            ybt_tiles[u] = ybt
 
-        def transpose_back(g):
+        def transpose_back(u):
+            ybp = psum.tile([P, 2, UT, D], F32, tag="ybp", bufs=2)
             for qk in range(2):
-                ybt = ybt_tiles[(g, qk)]
-                ybp = psum.tile([P, T, D], F32, tag="ybp", bufs=2)
-                for t in range(T):
-                    nc.tensor.transpose(ybp[:, t, :], ybt[:, t * P : (t + 1) * P], ident[:])
-                ybp_tiles[(g, qk)] = ybp
+                for tt in range(UT):
+                    tokens = ybt_tiles[u][:, qk, tt * P : (tt + 1) * P]
+                    if tt == 0:
+                        nc.tensor.matmul(out=ybp[:, qk, tt, :], lhsT=tokens, rhs=ident[:], start=True, stop=True)
+                    else:
+                        nc.tensor.transpose(ybp[:, qk, tt, :], tokens, ident[:])
+            ybp_tiles[u] = ybp
 
-        def norms(g):
-            ss = work.tile([P, 2 * T], F32, tag="ss", bufs=3)
+        def norms(u):
+            ss = work.tile([P, 2 * UT], F32, tag="ss", bufs=3)
             for qk in range(2):
-                for t in range(T):
+                for tt in range(UT):
                     squares = work.tile([P, D], F32, tag="squares", bufs=2)
                     nc.scalar.activation(
                         out=squares[:],
-                        in_=ybp_tiles[(g, qk)][:, t, :],
+                        in_=ybp_tiles[u][:, qk, tt, :],
                         func=ACT.Square,
-                        accum_out=ss[:, qk * T + t : qk * T + t + 1],
+                        accum_out=ss[:, qk * UT + tt : qk * UT + tt + 1],
                     )
-            rms = work.tile([P, 2 * T], F32, tag="rms", bufs=3)
-            nc.scalar.activation(out=rms[:], in_=ss[:], func=ACT.Sqrt, scale=1.0 / D, bias=EPS)
-            r = work.tile([P, 2 * T], F32, tag="r", bufs=3)
-            nc.vector.reciprocal(out=r[:], in_=rms[:])
-            r_tiles[g] = r
+            r = work.tile([P, 2 * UT], F32, tag="r", bufs=3)
+            nc.scalar.activation(out=r[:], in_=ss[:], func=ACT.Abs_reciprocal_sqrt, scale=1.0 / D, bias=EPS)
+            r_tiles[u] = r
 
-        def rotate_and_store(g):
+        def rotate(u, qk):
+            g, t0, _ = place(u)
+            block = g // BATCH
+            parts = []
+            for h, tag in ((0, "from_even%d" % qk), (1, "from_odd%d" % qk)):
+                part = work.tile([P, UT, D], F32, name=tag, tag=tag, bufs=3)
+                parts.append(part)
+            for tt in range(UT):
+                col = qk * UT + tt
+                pairs = ybp_tiles[u][:, qk, tt, :].rearrange("p (i h) -> p i h", h=2)
+                for h in range(2):
+                    nc.vector.scalar_tensor_tensor(
+                        out=parts[h][:, tt, :].rearrange("p (i h) -> p i h", h=2),
+                        in0=pairs[:, :, h : h + 1].to_broadcast([P, HALF, 2]),
+                        scalar=r_tiles[u][:, col : col + 1],
+                        in1=tables[(block, qk, h)][:, t0 + tt, :, :].rearrange("p h i -> p i h"),
+                        op0=ALU.mult,
+                        op1=ALU.mult,
+                    )
+            product_tiles[(u, qk)] = parts
+
+        def add_and_store(u, qk):
+            g, t0, _ = place(u)
             block, b = divmod(g, BATCH)
-            r = r_tiles[g]
-            for qk in range(2):
-                ybp = ybp_tiles[(g, qk)]
-                from_even = work.tile([P, T, D], F32, tag="from_even", bufs=4)
-                from_odd = work.tile([P, T, D], F32, tag="from_odd", bufs=4)
-                for t in range(T):
-                    col = qk * T + t
-                    pairs = ybp[:, t, :].rearrange("p (i h) -> p i h", h=2)
-                    for h, tabs, part in ((0, even_tabs, from_even), (1, odd_tabs, from_odd)):
-                        nc.vector.scalar_tensor_tensor(
-                            out=part[:, t, :].rearrange("p (i h) -> p i h", h=2),
-                            in0=pairs[:, :, h : h + 1].to_broadcast([P, HALF, 2]),
-                            scalar=r[:, col : col + 1],
-                            in1=tabs[(block, qk)][:, t, :, :].rearrange("p h i -> p i h"),
-                            op0=ALU.mult,
-                            op1=ALU.mult,
-                        )
-                result = work.tile([P, T, D], F32, tag="result", bufs=4)
-                nc.gpsimd.tensor_tensor(out=result[:], in0=from_even[:], in1=from_odd[:], op=ALU.add)
+            if t0 == 0:
+                result = work.tile([P, T, D], F32, name="result%d" % qk, tag="result%d" % qk, bufs=3)
+                result_tiles[(g, qk)] = result
+            result = result_tiles[(g, qk)]
+            from_even, from_odd = product_tiles[(u, qk)]
+            nc.gpsimd.tensor_tensor(
+                out=result[:, t0 : t0 + UT, :], in0=from_even[:], in1=from_odd[:], op=ALU.add
+            )
+            if t0 + UT == T:
                 nc.sync.dma_start(
                     out=outs[qk][b, block * BLOCK : (block + 1) * BLOCK, 0, :].rearrange("(p t) d -> p t d", t=T),
                     in_=result[:],
                 )
 
+        pending_tables = []
         with tc.manual_schedule():
-            for i in range(GROUPS + 3):
-                if i + LOOKAHEAD < GROUPS:
-                    load_x(i + LOOKAHEAD)
-                if 0 <= i - 3 < GROUPS:
-                    rotate_and_store(i - 3)
-                if 0 <= i - 2 < GROUPS:
-                    add_bias(i - 2)
-                if i < GROUPS:
-                    transpose_x(i)
-                if i == 0:
-                    spread_vectors()
+            for s in range(UNITS + 5):
+                if s % UNITS_PER_GROUP == 0:
+                    g = s // UNITS_PER_GROUP + LOOKAHEAD
+                    if g < GROUPS:
+                        fetch(load_x(g))
+                if 0 <= s - 1 < UNITS:
+                    quantise_x(s - 1)
+                if 0 <= s - 3 < UNITS:
+                    rotate(s - 3, 0)
+                    add_and_store(s - 3, 0)
+                if 0 <= s - 4 < UNITS:
+                    add_and_store(s - 4, 1)
+                if 0 <= s - 2 < UNITS:
+                    add_bias(s - 2)
+                if s < UNITS:
+                    transpose_x(s)
+                    copy_x(s, 0, nc.scalar.copy)
+                    copy_x(s, 1, nc.scalar.copy if s % 4 == 3 else nc.vector.tensor_copy)
+                if s == 0:
                     quantise_weights(0)
+                    spread_vectors()
                     for qk in range(2):
-                        build_tables(0, qk)
-                if i == 3:
+                        for step in table_steps(0, qk):
+                            build_table(step)
+                    for block in range(1, BLOCKS):
+                        for qk in range(2):
+                            pending_tables.extend(table_steps(block, qk))
+                if s == 5:
                     quantise_weights(1)
-                if i % BATCH < 2 and i // BATCH + 1 < BLOCKS:
-                    build_tables(i // BATCH + 1, i % BATCH)
-                if 0 <= i - 2 < GROUPS:
-                    transpose_back(i - 2)
-                if 0 <= i - 1 < GROUPS:
-                    project(i - 1)
-                if i < GROUPS:
-                    quantise_x(i)
-                if 0 <= i - 2 < GROUPS:
-                    norms(i - 2)
+                if s >= 2:
+                    for step in pending_tables[:2]:
+                        build_table(step)
+                    pending_tables = pending_tables[2:]
+                if 0 <= s - 2 < UNITS:
+                    transpose_back(s - 2)
+                if 0 <= s - 1 < UNITS:
+                    project(s - 1)
+                if 0 <= s - 3 < UNITS:
+                    rotate(s - 3, 1)
+                if 0 <= s - 2 < UNITS:
+                    norms(s - 2)

@@ -21,11 +21,9 @@ BLOCK = 512
 T = BLOCK // P
 BLOCKS = 4
 GROUPS = BLOCKS * BATCH
-UT = 2
-UNIT = UT * P
-UNITS_PER_GROUP = T // UT
-UNITS = GROUPS * UNITS_PER_GROUP
-UNITS_PER_BLOCK = UNITS // BLOCKS
+STEPS = 2 * GROUPS
+XT = T // 2
+XHALF = XT * P
 PASSES = K // 512
 WORD_TILES = K // 2 // P
 LOOKAHEAD = 5
@@ -72,8 +70,8 @@ def tile_fluxjointattention_pa_t_kernel(
         ybt_tiles = {}
         ybp_tiles = {}
         r_tiles = {}
-        product_tiles = {}
-        result_tiles = {}
+        xt_tiles = {}
+        parts_tiles = {}
 
         def load_x(g, pieces=1):
             block, b = divmod(g, BATCH)
@@ -122,7 +120,7 @@ def tile_fluxjointattention_pa_t_kernel(
                 )
             w_raw[stream] = raw
 
-        first_x = load_x(0, UNITS_PER_GROUP)
+        first_x = load_x(0, 2)
         fetch(first_x[:1])
         load_weights(0)
         fetch(first_x[1:])
@@ -159,10 +157,10 @@ def tile_fluxjointattention_pa_t_kernel(
         gain_pairs = consts.tile([P, 4, 3, HALF], F32)
 
         def spread_vectors():
-            bias_ps = psum.tile([P, P], BF16, tag="ybp", bufs=2)
+            bias_ps = psum.tile([P, P], BF16, tag="ybp", bufs=3)
             nc.tensor.transpose(bias_ps[:], bias_rows[:], ident_bf[:])
             nc.vector.tensor_copy(out=bias_col[:], in_=bias_ps[:, 0:4])
-            gain_ps = psum.tile([P, 4 * D], F32, tag="ybp", bufs=2)
+            gain_ps = psum.tile([P, 4 * D], F32, tag="ybp", bufs=3)
             nc.tensor.matmul(out=gain_ps[:], lhsT=ones[:], rhs=gain_rows[:], start=True, stop=True)
             nc.vector.tensor_copy(
                 out=gain_pairs[:, :, 0:2, :], in_=gain_ps[:].rearrange("p (j i h) -> p j h i", j=4, h=2)
@@ -175,176 +173,165 @@ def tile_fluxjointattention_pa_t_kernel(
             j = 2 * min(block, 1) + qk
             cos_pairs = cos_sb[:, block, :].rearrange("p (t i h) -> p t h i", t=T, h=2)
             sin_pairs = sin_sb[:, block, :].rearrange("p (t i h) -> p t h i", t=T, h=2)
-            even_tab = consts.tile([P, T, 2, HALF], F32, name="even_tab%d_%d" % (block, qk))
-            odd_tab = consts.tile([P, T, 2, HALF], F32, name="odd_tab%d_%d" % (block, qk))
-            tables[(block, qk, 0)] = even_tab
-            tables[(block, qk, 1)] = odd_tab
+            table = consts.tile([P, T, 2, 2, HALF], F32, name="table%d_%d" % (block, qk))
+            tables[(block, qk)] = table
             return [
-                (table, h, angles, gain_pairs[:, j, gain, :])
-                for table, h, angles, gain in (
-                    (even_tab, 0, cos_pairs, 0),
-                    (even_tab, 1, sin_pairs, 0),
-                    (odd_tab, 0, sin_pairs, 2),
-                    (odd_tab, 1, cos_pairs, 1),
+                (table[:, :, s, h, :], angles[:, :, h, :], gain_pairs[:, j, gain, :])
+                for s, h, angles, gain in (
+                    (0, 0, cos_pairs, 0),
+                    (0, 1, sin_pairs, 0),
+                    (1, 0, sin_pairs, 2),
+                    (1, 1, cos_pairs, 1),
                 )
             ]
 
         def build_table(step):
-            table, h, angles, gain = step
+            factors, angles, gain = step
             nc.gpsimd.tensor_tensor(
-                out=table[:, :, h, :],
-                in0=angles[:, :, h, :],
+                out=factors,
+                in0=angles,
                 in1=gain.unsqueeze(1).to_broadcast([P, T, HALF]),
                 op=ALU.mult,
             )
 
-        def place(u):
-            g, half = divmod(u, UNITS_PER_GROUP)
-            return g, half * UT, min(g // BATCH, 1)
+        def place(m):
+            g, qk = divmod(m, 2)
+            return g, qk, min(g // BATCH, 1)
 
-        def transpose_x(u):
-            g, t0, _ = place(u)
+        def transpose_x(j, tt):
+            g, half = divmod(j, 2)
             x_words = x_tiles[g][:].bitcast(F32)
-            banks = []
-            for tt in range(UT):
-                xt = psum.tile([P, WORD_TILES, P], F32, tag="xt", bufs=4)
-                for a in range(WORD_TILES):
-                    c, w = divmod(a, 2)
-                    first = (t0 + tt) * (K // 2) + c * 2 * P
-                    nc.tensor.transpose(xt[:, a, :], x_words[:, first + w : first + 2 * P : 2], ident[:])
-                banks.append(xt)
-            grouped = work.tile([P, PASSES * UNIT * 4], BF16, tag="grouped", bufs=3, align_bytes=64)
-            grouped_tiles[u] = (grouped, banks)
+            xt = psum.tile([P, WORD_TILES, P], F32, tag="xt", bufs=3)
+            for a in range(WORD_TILES):
+                c, w = divmod(a, 2)
+                first = (half * XT + tt) * (K // 2) + c * 2 * P
+                nc.tensor.transpose(xt[:, a, :], x_words[:, first + w : first + 2 * P : 2], ident[:])
+            xt_tiles[(j, tt)] = xt
 
-        def copy_x(u, tt, copy_out):
-            grouped, banks = grouped_tiles[u]
-            words = grouped[:].bitcast(F32).rearrange("p (c n w) -> p c n w", c=PASSES, w=2)
+        def copy_x(j, tt, copy_out):
+            if tt == 0:
+                grouped = work.tile([P, PASSES * XHALF * 4], BF16, tag="grouped", bufs=3, align_bytes=64)
+                grouped_tiles[j] = grouped
+            words = grouped_tiles[j][:].bitcast(F32).rearrange("p (c n w) -> p c n w", c=PASSES, w=2)
             copy_out(
                 out=words[:, :, tt * P : (tt + 1) * P, :],
-                in_=banks[tt][:].rearrange("p (c w) n -> p c n w", c=PASSES),
+                in_=xt_tiles[(j, tt)][:].rearrange("p (c w) n -> p c n w", c=PASSES),
             )
 
-        def quantise_x(u):
-            grouped, _ = grouped_tiles[u]
-            codes = work.tile([P, PASSES * UNIT], U32, tag="codes", bufs=3, align_bytes=64)
-            scales = work.tile([P, PASSES * UNIT], U8, tag="scales", bufs=3, align_bytes=64)
-            nc.vector.quantize_mx(out=codes[:].bitcast(FP8X4), scales=scales[:], in_=grouped[:])
-            mx_tiles[u] = (codes, scales)
+        def quantise_x(j):
+            codes = work.tile([P, PASSES * XHALF], U32, tag="codes", bufs=5, align_bytes=64)
+            scales = work.tile([P, PASSES * XHALF], U8, tag="scales", bufs=5, align_bytes=64)
+            nc.vector.quantize_mx(out=codes[:].bitcast(FP8X4), scales=scales[:], in_=grouped_tiles[j][:])
+            mx_tiles[j] = (codes, scales)
 
-        def project(u):
-            _, _, stream = place(u)
-            codes, scales = mx_tiles[u]
-            yt = psum.tile([P, 2, UNIT], F32, tag="yt", bufs=2)
-            for qk in range(2):
-                for c in range(PASSES):
-                    w_cols = slice((2 * qk + c) * P, (2 * qk + c + 1) * P)
-                    x_cols = slice(c * UNIT, (c + 1) * UNIT)
-                    nc.tensor.matmul_mx(
-                        out=yt[:, qk, :],
-                        lhsT=w_codes[stream][:, w_cols].bitcast(FP8X4),
-                        lhsT_scale=w_scales[stream][:, w_cols],
-                        rhs=codes[:, x_cols].bitcast(FP8X4),
-                        rhs_scale=scales[:, x_cols],
-                        start=(c == 0),
-                        stop=(c == PASSES - 1),
-                    )
-            yt_tiles[u] = yt
-
-        def add_bias(u):
-            _, _, stream = place(u)
-            ybt = work.tile([P, 2, UNIT], F32, tag="ybt", bufs=3)
-            for qk in range(2):
-                j = 2 * stream + qk
-                nc.scalar.activation(
-                    out=ybt[:, qk, :], in_=yt_tiles[u][:, qk, :], func=ACT.Identity, bias=bias_col[:, j : j + 1]
+        def project(m, half):
+            g, qk, stream = place(m)
+            codes, scales = mx_tiles[2 * g + half]
+            if half == 0:
+                yt = psum.tile([P, 2, XHALF], F32, tag="yt", bufs=2)
+                yt_tiles[m] = yt
+            for c in range(PASSES):
+                w_cols = slice((2 * qk + c) * P, (2 * qk + c + 1) * P)
+                x_cols = slice(c * XHALF, (c + 1) * XHALF)
+                nc.tensor.matmul_mx(
+                    out=yt_tiles[m][:, half, :],
+                    lhsT=w_codes[stream][:, w_cols].bitcast(FP8X4),
+                    lhsT_scale=w_scales[stream][:, w_cols],
+                    rhs=codes[:, x_cols].bitcast(FP8X4),
+                    rhs_scale=scales[:, x_cols],
+                    start=(c == 0),
+                    stop=(c == PASSES - 1),
                 )
-            ybt_tiles[u] = ybt
 
-        def transpose_back(u):
-            ybp = psum.tile([P, 2, UT, D], F32, tag="ybp", bufs=2)
-            for qk in range(2):
-                for tt in range(UT):
-                    tokens = ybt_tiles[u][:, qk, tt * P : (tt + 1) * P]
-                    if tt == 0:
-                        nc.tensor.matmul(out=ybp[:, qk, tt, :], lhsT=tokens, rhs=ident[:], start=True, stop=True)
-                    else:
-                        nc.tensor.transpose(ybp[:, qk, tt, :], tokens, ident[:])
-            ybp_tiles[u] = ybp
+        def add_bias(m):
+            _, qk, stream = place(m)
+            col = 2 * stream + qk
+            ybt = work.tile([P, T, P], F32, tag="ybt", bufs=3)
+            nc.scalar.activation(
+                out=ybt[:].rearrange("p t n -> p (t n)"),
+                in_=yt_tiles[m][:].rearrange("p h n -> p (h n)"),
+                func=ACT.Identity,
+                bias=bias_col[:, col : col + 1],
+            )
+            ybt_tiles[m] = ybt
 
-        def norms(u):
-            ss = work.tile([P, 2 * UT], F32, tag="ss", bufs=3)
-            for qk in range(2):
-                for tt in range(UT):
-                    squares = work.tile([P, D], F32, tag="squares", bufs=2)
-                    nc.scalar.activation(
-                        out=squares[:],
-                        in_=ybp_tiles[u][:, qk, tt, :],
-                        func=ACT.Square,
-                        accum_out=ss[:, qk * UT + tt : qk * UT + tt + 1],
-                    )
-            r = work.tile([P, 2 * UT], F32, tag="r", bufs=3)
+        def transpose_back(m, half):
+            if half == 0:
+                ybp = psum.tile([P, T, D], F32, tag="ybp", bufs=3)
+                ybp_tiles[m] = ybp
+            ybp = ybp_tiles[m]
+            for t in range(half * XT, (half + 1) * XT):
+                tokens = ybt_tiles[m][:, t, :]
+                if t % 2 == 0:
+                    nc.tensor.matmul(out=ybp[:, t, :], lhsT=tokens, rhs=ident[:], start=True, stop=True)
+                else:
+                    nc.tensor.transpose(ybp[:, t, :], tokens, ident[:])
+
+        def norms(m):
+            ss = work.tile([P, T], F32, tag="ss", bufs=3)
+            for t in range(T):
+                squares = work.tile([P, D], F32, tag="squares", bufs=2)
+                nc.scalar.activation(
+                    out=squares[:], in_=ybp_tiles[m][:, t, :], func=ACT.Square, accum_out=ss[:, t : t + 1]
+                )
+            r = work.tile([P, T], F32, tag="r", bufs=3)
             nc.scalar.activation(out=r[:], in_=ss[:], func=ACT.Abs_reciprocal_sqrt, scale=1.0 / D, bias=EPS)
-            r_tiles[u] = r
+            r_tiles[m] = r
 
-        def rotate(u, qk):
-            g, t0, _ = place(u)
-            block = g // BATCH
-            parts = []
-            for h, tag in ((0, "from_even%d" % qk), (1, "from_odd%d" % qk)):
-                part = work.tile([P, UT, D], F32, name=tag, tag=tag, bufs=3)
-                parts.append(part)
-            for tt in range(UT):
-                col = qk * UT + tt
-                pairs = ybp_tiles[u][:, qk, tt, :].rearrange("p (i h) -> p i h", h=2)
-                for h in range(2):
+        def rotate(m, half):
+            g, qk, _ = place(m)
+            if half == 0:
+                parts = work.tile([P, 2, T, D], F32, tag="parts", bufs=4)
+                parts_tiles[m] = parts
+            parts = parts_tiles[m]
+            for t in range(half * XT, (half + 1) * XT):
+                pairs = ybp_tiles[m][:, t, :].rearrange("p (i s) -> p i s", s=2)
+                for s in range(2):
                     nc.vector.scalar_tensor_tensor(
-                        out=parts[h][:, tt, :].rearrange("p (i h) -> p i h", h=2),
-                        in0=pairs[:, :, h : h + 1].to_broadcast([P, HALF, 2]),
-                        scalar=r_tiles[u][:, col : col + 1],
-                        in1=tables[(block, qk, h)][:, t0 + tt, :, :].rearrange("p h i -> p i h"),
+                        out=parts[:, s, t, :].rearrange("p (i h) -> p i h", h=2),
+                        in0=pairs[:, :, s : s + 1].to_broadcast([P, HALF, 2]),
+                        scalar=r_tiles[m][:, t : t + 1],
+                        in1=tables[(g // BATCH, qk)][:, t, s, :, :].rearrange("p h i -> p i h"),
                         op0=ALU.mult,
                         op1=ALU.mult,
                     )
-            product_tiles[(u, qk)] = parts
 
-        def add_and_store(u, qk):
-            g, t0, _ = place(u)
+        def add_and_store(m):
+            g, qk, _ = place(m)
             block, b = divmod(g, BATCH)
-            if t0 == 0:
-                result = work.tile([P, T, D], F32, name="result%d" % qk, tag="result%d" % qk, bufs=3)
-                result_tiles[(g, qk)] = result
-            result = result_tiles[(g, qk)]
-            from_even, from_odd = product_tiles[(u, qk)]
-            nc.gpsimd.tensor_tensor(
-                out=result[:, t0 : t0 + UT, :], in0=from_even[:], in1=from_odd[:], op=ALU.add
+            parts = parts_tiles[m]
+            result = work.tile([P, T, D], F32, tag="result", bufs=4)
+            nc.gpsimd.tensor_tensor(out=result[:], in0=parts[:, 0, :, :], in1=parts[:, 1, :, :], op=ALU.add)
+            nc.sync.dma_start(
+                out=outs[qk][b, block * BLOCK : (block + 1) * BLOCK, 0, :].rearrange("(p t) d -> p t d", t=T),
+                in_=result[:],
             )
-            if t0 + UT == T:
-                nc.sync.dma_start(
-                    out=outs[qk][b, block * BLOCK : (block + 1) * BLOCK, 0, :].rearrange("(p t) d -> p t d", t=T),
-                    in_=result[:],
-                )
 
         pending_tables = []
         with tc.manual_schedule():
-            for s in range(UNITS + 5):
-                if s % UNITS_PER_GROUP == 0:
-                    g = s // UNITS_PER_GROUP + LOOKAHEAD
-                    if g < GROUPS:
-                        fetch(load_x(g))
-                if 0 <= s - 1 < UNITS:
-                    quantise_x(s - 1)
-                if 0 <= s - 3 < UNITS:
-                    rotate(s - 3, 0)
-                    add_and_store(s - 3, 0)
-                if 0 <= s - 4 < UNITS:
-                    add_and_store(s - 4, 1)
-                if 0 <= s - 2 < UNITS:
-                    add_bias(s - 2)
-                if s < UNITS:
-                    transpose_x(s)
-                    copy_x(s, 0, nc.scalar.copy)
-                    copy_x(s, 1, nc.scalar.copy if s % 4 == 3 else nc.vector.tensor_copy)
-                if s == 0:
+            for j in range(STEPS + 7):
+                if j % 2 == 0 and j // 2 + LOOKAHEAD < GROUPS:
+                    fetch(load_x(j // 2 + LOOKAHEAD))
+                if 0 <= j - 4 < STEPS:
+                    add_bias(j - 4)
+                if 0 <= j - 6 < STEPS:
+                    rotate(j - 6, 0)
+                if 0 <= j - 1 < STEPS:
+                    quantise_x(j - 1)
+                if 0 <= j - 6 < STEPS:
+                    rotate(j - 6, 1)
+                    add_and_store(j - 6)
+                for half in range(2):
+                    if j < STEPS:
+                        transpose_x(j, half)
+                    if 0 <= j - 5 < STEPS:
+                        transpose_back(j - 5, half)
+                    if 0 <= j - 3 < STEPS:
+                        project(j - 3, half)
+                if j < STEPS:
+                    copy_x(j, 0, nc.scalar.copy)
+                    copy_x(j, 1, nc.scalar.copy if j % 4 == 3 else nc.vector.tensor_copy)
+                if j == 0:
                     quantise_weights(0)
                     spread_vectors()
                     for qk in range(2):
@@ -353,17 +340,11 @@ def tile_fluxjointattention_pa_t_kernel(
                     for block in range(1, BLOCKS):
                         for qk in range(2):
                             pending_tables.extend(table_steps(block, qk))
-                if s == 5:
+                if j == 5:
                     quantise_weights(1)
-                if s >= 2:
+                if j >= 2:
                     for step in pending_tables[:2]:
                         build_table(step)
                     pending_tables = pending_tables[2:]
-                if 0 <= s - 2 < UNITS:
-                    transpose_back(s - 2)
-                if 0 <= s - 1 < UNITS:
-                    project(s - 1)
-                if 0 <= s - 3 < UNITS:
-                    rotate(s - 3, 1)
-                if 0 <= s - 2 < UNITS:
-                    norms(s - 2)
+                if 0 <= j - 5 < STEPS:
+                    norms(j - 5)

@@ -326,13 +326,12 @@ def tile_fluxjointattention_pa_t_kernel(
                         transpose_x(j, half)
                     if 0 <= j - 5 < STEPS:
                         transpose_back(j - 5, half)
-                    if 0 <= j - 3 < STEPS:
-                        project(j - 3, half)
                 if j < STEPS:
                     copy_x(j, 0, nc.scalar.copy)
                     copy_x(j, 1, nc.scalar.copy if j % 4 == 3 else nc.vector.tensor_copy)
                 if j == 0:
                     quantise_weights(0)
+                if j == 2:
                     spread_vectors()
                     for qk in range(2):
                         for step in table_steps(0, qk):
@@ -346,5 +345,8 @@ def tile_fluxjointattention_pa_t_kernel(
                     for step in pending_tables[:2]:
                         build_table(step)
                     pending_tables = pending_tables[2:]
+                if 0 <= j - 3 < STEPS:
+                    for half in range(2):
+                        project(j - 3, half)
                 if 0 <= j - 5 < STEPS:
                     norms(j - 5)

@@ -26,6 +26,7 @@ XT = T // 2
 XHALF = XT * P
 PASSES = K // 512
 WORD_TILES = K // 2 // P
+TABLES_AHEAD = 16
 LOOKAHEAD = 5
 
 FLOPS = 2 * BATCH * BLOCKS * BLOCK * K * 2 * D
@@ -120,20 +121,28 @@ def tile_fluxjointattention_pa_t_kernel(
                 )
             w_raw[stream] = raw
 
+        cos_sb = consts.tile([P, BLOCKS, T * D], BF16)
+        sin_sb = consts.tile([P, BLOCKS, T * D], BF16)
+
+        def load_angles(blocks):
+            for tile, source in ((cos_sb, rope_cos), (sin_sb, rope_sin)):
+                nc.sync.dma_start(
+                    out=tile[:, blocks, :],
+                    in_=source.rearrange("(c p t) d -> p c (t d)", c=BLOCKS, p=P, t=T)[:, blocks, :],
+                )
+
         first_x = load_x(0, 2)
         fetch(first_x[:1])
         load_weights(0)
+        for j in range(4):
+            nc.scalar.dma_start(out=gain_rows[0:1, j * D : (j + 1) * D], in_=gains[j].unsqueeze(0))
         fetch(first_x[1:])
         for j in range(4):
             nc.scalar.dma_start(out=bias_rows[j : j + 1, :], in_=biases[j].unsqueeze(0))
-        for j in range(4):
-            nc.scalar.dma_start(out=gain_rows[0:1, j * D : (j + 1) * D], in_=gains[j].unsqueeze(0))
         fetch(load_x(1))
-        cos_sb = consts.tile([P, BLOCKS, T * D], BF16)
-        nc.sync.dma_start(out=cos_sb[:], in_=rope_cos.rearrange("(c p t) d -> p c (t d)", c=BLOCKS, p=P, t=T))
-        sin_sb = consts.tile([P, BLOCKS, T * D], BF16)
-        nc.sync.dma_start(out=sin_sb[:], in_=rope_sin.rearrange("(c p t) d -> p c (t d)", c=BLOCKS, p=P, t=T))
+        load_angles(slice(0, 1))
         fetch(load_x(2))
+        load_angles(slice(1, BLOCKS))
         fetch(load_x(3))
         load_weights(1)
         fetch(load_x(4))
@@ -278,23 +287,20 @@ def tile_fluxjointattention_pa_t_kernel(
             nc.scalar.activation(out=r[:], in_=ss[:], func=ACT.Abs_reciprocal_sqrt, scale=1.0 / D, bias=EPS)
             r_tiles[m] = r
 
-        def rotate(m, half):
+        def rotate(m, pieces):
             g, qk, _ = place(m)
-            if half == 0:
+            if m not in parts_tiles:
                 parts = work.tile([P, 2, T, D], F32, tag="parts", bufs=4)
                 parts_tiles[m] = parts
-            parts = parts_tiles[m]
-            for t in range(half * XT, (half + 1) * XT):
-                pairs = ybp_tiles[m][:, t, :].rearrange("p (i s) -> p i s", s=2)
-                for s in range(2):
-                    nc.vector.scalar_tensor_tensor(
-                        out=parts[:, s, t, :].rearrange("p (i h) -> p i h", h=2),
-                        in0=pairs[:, :, s : s + 1].to_broadcast([P, HALF, 2]),
-                        scalar=r_tiles[m][:, t : t + 1],
-                        in1=tables[(g // BATCH, qk)][:, t, s, :, :].rearrange("p h i -> p i h"),
-                        op0=ALU.mult,
-                        op1=ALU.mult,
-                    )
+            for t, s in pieces:
+                nc.vector.scalar_tensor_tensor(
+                    out=parts_tiles[m][:, s, t, :].rearrange("p (i h) -> p i h", h=2),
+                    in0=ybp_tiles[m][:, t, :].rearrange("p (i s) -> p i s", s=2)[:, :, s : s + 1].to_broadcast([P, HALF, 2]),
+                    scalar=r_tiles[m][:, t : t + 1],
+                    in1=tables[(g // BATCH, qk)][:, t, s, :, :].rearrange("p h i -> p i h"),
+                    op0=ALU.mult,
+                    op1=ALU.mult,
+                )
 
         def add_and_store(m):
             g, qk, _ = place(m)
@@ -307,46 +313,47 @@ def tile_fluxjointattention_pa_t_kernel(
                 in_=result[:],
             )
 
+        pieces = [(t, s) for t in range(T) for s in range(2)]
         pending_tables = []
         with tc.manual_schedule():
             for j in range(STEPS + 7):
                 if j % 2 == 0 and j // 2 + LOOKAHEAD < GROUPS:
                     fetch(load_x(j // 2 + LOOKAHEAD))
-                if 0 <= j - 4 < STEPS:
-                    add_bias(j - 4)
-                if 0 <= j - 6 < STEPS:
-                    rotate(j - 6, 0)
+                if j == 0:
+                    quantise_weights(0)
+                if 0 <= j - 3 < STEPS:
+                    add_bias(j - 3)
                 if 0 <= j - 1 < STEPS:
                     quantise_x(j - 1)
                 if 0 <= j - 6 < STEPS:
-                    rotate(j - 6, 1)
+                    rotate(j - 6, pieces[-1:])
                     add_and_store(j - 6)
+                if 0 <= j - 5 < STEPS:
+                    rotate(j - 5, pieces[:-2])
                 for half in range(2):
                     if j < STEPS:
                         transpose_x(j, half)
-                    if 0 <= j - 5 < STEPS:
-                        transpose_back(j - 5, half)
+                    if 0 <= j - 4 < STEPS:
+                        transpose_back(j - 4, half)
                 if j < STEPS:
                     copy_x(j, 0, nc.scalar.copy)
-                    copy_x(j, 1, nc.scalar.copy if j % 4 == 3 else nc.vector.tensor_copy)
-                if j == 0:
-                    quantise_weights(0)
-                if j == 2:
+                    copy_x(j, 1, nc.scalar.copy if j % 2 else nc.vector.tensor_copy)
+                if 0 <= j - 5 < STEPS:
+                    rotate(j - 5, pieces[-2:-1])
+                if j == 1:
                     spread_vectors()
-                    for qk in range(2):
-                        for step in table_steps(0, qk):
-                            build_table(step)
-                    for block in range(1, BLOCKS):
+                    for block in range(BLOCKS):
                         for qk in range(2):
                             pending_tables.extend(table_steps(block, qk))
+                    for step in pending_tables[:TABLES_AHEAD]:
+                        build_table(step)
+                    pending_tables = pending_tables[TABLES_AHEAD:]
                 if j == 5:
                     quantise_weights(1)
-                if j >= 2:
-                    for step in pending_tables[:2]:
-                        build_table(step)
-                    pending_tables = pending_tables[2:]
-                if 0 <= j - 3 < STEPS:
+                if j >= 6 and pending_tables:
+                    build_table(pending_tables.pop(0))
+                if 0 <= j - 2 < STEPS:
                     for half in range(2):
-                        project(j - 3, half)
-                if 0 <= j - 5 < STEPS:
-                    norms(j - 5)
+                        project(j - 2, half)
+                if 0 <= j - 4 < STEPS:
+                    norms(j - 4)

from contextlib import ExitStack

import concourse.mybir as mybir
from concourse.masks import make_identity

F32 = mybir.dt.float32
BF16 = mybir.dt.bfloat16
U32 = mybir.dt.uint32
U8 = mybir.dt.uint8
FP8X4 = mybir.dt.float8_e4m3fn_x4
ACT = mybir.ActivationFunctionType
ALU = mybir.AluOpType

P = 128
BATCH = 4
K = 1024
D = 128
HALF = D // 2
EPS = 1e-6
BLOCK = 512
T = BLOCK // P
BLOCKS = 4
GROUPS = BLOCKS * BATCH
STEPS = 2 * GROUPS
XT = T // 2
XHALF = XT * P
PASSES = K // 512
WORD_TILES = K // 2 // P
TABLES_AHEAD = 16
LOOKAHEAD = 5

FLOPS = 2 * BATCH * BLOCKS * BLOCK * K * 2 * D


def tile_fluxjointattention_pa_t_kernel(
    tc,
    hidden_states,
    encoder_hidden_states,
    rope_cos,
    rope_sin,
    Wq,
    Wk,
    Waq,
    Wak,
    bq,
    bk,
    baq,
    bak,
    g_q,
    g_k,
    g_aq,
    g_ak,
    out_0,
    out_1,
):
    nc = tc.nc
    outs = (out_0, out_1)
    weights = (Waq, Wak, Wq, Wk)
    biases = (baq, bak, bq, bk)
    gains = (g_aq, g_ak, g_q, g_k)

    with ExitStack() as ctx:
        consts = ctx.enter_context(tc.tile_pool(name="consts", bufs=1))
        work = ctx.enter_context(tc.tile_pool(name="work", bufs=2))
        psum = ctx.enter_context(tc.psum_pool(name="psum", bufs=1))

        x_tiles = {}
        grouped_tiles = {}
        mx_tiles = {}
        yt_tiles = {}
        ybt_tiles = {}
        ybp_tiles = {}
        r_tiles = {}
        xt_tiles = {}
        parts_tiles = {}

        def load_x(g, pieces=1):
            block, b = divmod(g, BATCH)
            if block == 0:
                rows = encoder_hidden_states[b]
            else:
                rows = hidden_states[b, (block - 1) * BLOCK : block * BLOCK, :]
            rows = rows.rearrange("(p t) k -> p (t k)", t=T)
            if g not in x_tiles:
                x_sb = work.tile([P, T * K], BF16, tag="x", bufs=LOOKAHEAD + 2)
                x_tiles[g] = x_sb
            return [
                (x_tiles[g][:, c * T * K // pieces : (c + 1) * T * K // pieces],
                 rows[:, c * T * K // pieces : (c + 1) * T * K // pieces])
                for c in range(pieces)
            ]

        def fetch(pairs):
            for dst, src in pairs:
                nc.sync.dma_start(out=dst, in_=src)

        warm = consts.tile([P, 1], F32)
        nc.vector.memset(warm[:], 1.0)
        nc.scalar.activation(out=warm[:], in_=warm[:], func=ACT.Abs_reciprocal_sqrt)

        bias_rows = consts.tile([P, P], BF16)
        nc.vector.memset(bias_rows[:], 0.0)
        gain_rows = consts.tile([P, 4 * D], BF16)
        nc.vector.memset(gain_rows[:], 0.0)
        ones = consts.tile([P, P], BF16)
        nc.vector.memset(ones[:], 1.0)

        ident = consts.tile([P, P], F32)
        make_identity(nc, ident[:])
        ident_bf = consts.tile([P, P], BF16)
        nc.vector.tensor_copy(out=ident_bf[:], in_=ident[:])

        w_raw = {}

        def load_weights(stream):
            raw = consts.tile([P, 2 * K * D // P], BF16, name="w_raw%d" % stream)
            for qk in range(2):
                nc.sync.dma_start(
                    out=raw[:, qk * 1024 : (qk + 1) * 1024].rearrange("p (c f) -> p c f", c=PASSES),
                    in_=weights[2 * stream + qk].rearrange("(c p j) n -> p c (j n)", c=PASSES, p=P, j=4),
                )
            w_raw[stream] = raw

        cos_sb = consts.tile([P, BLOCKS, T * D], BF16)
        sin_sb = consts.tile([P, BLOCKS, T * D], BF16)

        def load_angles(blocks):
            for tile, source in ((cos_sb, rope_cos), (sin_sb, rope_sin)):
                nc.sync.dma_start(
                    out=tile[:, blocks, :],
                    in_=source.rearrange("(c p t) d -> p c (t d)", c=BLOCKS, p=P, t=T)[:, blocks, :],
                )

        first_x = load_x(0, 2)
        fetch(first_x[:1])
        load_weights(0)
        for j in range(4):
            nc.scalar.dma_start(out=gain_rows[0:1, j * D : (j + 1) * D], in_=gains[j].unsqueeze(0))
        fetch(first_x[1:])
        for j in range(4):
            nc.scalar.dma_start(out=bias_rows[j : j + 1, :], in_=biases[j].unsqueeze(0))
        fetch(load_x(1))
        load_angles(slice(0, 1))
        fetch(load_x(2))
        load_angles(slice(1, BLOCKS))
        fetch(load_x(3))
        load_weights(1)
        fetch(load_x(4))

        w_codes = {}
        w_scales = {}

        def quantise_weights(stream):
            grouped = consts.tile([P, 2048], BF16, name="w_grouped%d" % stream, align_bytes=64)
            nc.vector.tensor_copy(
                out=grouped[:].rearrange("p (m n j) -> p m n j", m=4, j=4),
                in_=w_raw[stream][:].rearrange("p (m j n) -> p m n j", m=4, j=4),
            )
            codes = consts.tile([P, 512], U32, name="w_codes%d" % stream, align_bytes=64)
            scales = consts.tile([P, 512], U8, name="w_scales%d" % stream, align_bytes=64)
            nc.vector.quantize_mx(out=codes[:].bitcast(FP8X4), scales=scales[:], in_=grouped[:])
            w_codes[stream] = codes
            w_scales[stream] = scales

        bias_col = consts.tile([P, 4], F32)
        gain_pairs = consts.tile([P, 4, 3, HALF], F32)

        def spread_vectors():
            bias_ps = psum.tile([P, P], BF16, tag="ybp", bufs=3)
            nc.tensor.transpose(bias_ps[:], bias_rows[:], ident_bf[:])
            nc.vector.tensor_copy(out=bias_col[:], in_=bias_ps[:, 0:4])
            gain_ps = psum.tile([P, 4 * D], F32, tag="ybp", bufs=3)
            nc.tensor.matmul(out=gain_ps[:], lhsT=ones[:], rhs=gain_rows[:], start=True, stop=True)
            nc.vector.tensor_copy(
                out=gain_pairs[:, :, 0:2, :], in_=gain_ps[:].rearrange("p (j i h) -> p j h i", j=4, h=2)
            )
            nc.vector.tensor_scalar_mul(out=gain_pairs[:, :, 2, :], in0=gain_pairs[:, :, 1, :], scalar1=-1.0)

        tables = {}

        def table_steps(block, qk):
            j = 2 * min(block, 1) + qk
            cos_pairs = cos_sb[:, block, :].rearrange("p (t i h) -> p t h i", t=T, h=2)
            sin_pairs = sin_sb[:, block, :].rearrange("p (t i h) -> p t h i", t=T, h=2)
            table = consts.tile([P, T, 2, 2, HALF], F32, name="table%d_%d" % (block, qk))
            tables[(block, qk)] = table
            return [
                (table[:, :, s, h, :], angles[:, :, h, :], gain_pairs[:, j, gain, :])
                for s, h, angles, gain in (
                    (0, 0, cos_pairs, 0),
                    (0, 1, sin_pairs, 0),
                    (1, 0, sin_pairs, 2),
                    (1, 1, cos_pairs, 1),
                )
            ]

        def build_table(step):
            factors, angles, gain = step
            nc.gpsimd.tensor_tensor(
                out=factors,
                in0=angles,
                in1=gain.unsqueeze(1).to_broadcast([P, T, HALF]),
                op=ALU.mult,
            )

        def place(m):
            g, qk = divmod(m, 2)
            return g, qk, min(g // BATCH, 1)

        def transpose_x(j, tt):
            g, half = divmod(j, 2)
            x_words = x_tiles[g][:].bitcast(F32)
            xt = psum.tile([P, WORD_TILES, P], F32, tag="xt", bufs=3)
            for a in range(WORD_TILES):
                c, w = divmod(a, 2)
                first = (half * XT + tt) * (K // 2) + c * 2 * P
                nc.tensor.transpose(xt[:, a, :], x_words[:, first + w : first + 2 * P : 2], ident[:])
            xt_tiles[(j, tt)] = xt

        def copy_x(j, tt, copy_out):
            if tt == 0:
                grouped = work.tile([P, PASSES * XHALF * 4], BF16, tag="grouped", bufs=3, align_bytes=64)
                grouped_tiles[j] = grouped
            words = grouped_tiles[j][:].bitcast(F32).rearrange("p (c n w) -> p c n w", c=PASSES, w=2)
            copy_out(
                out=words[:, :, tt * P : (tt + 1) * P, :],
                in_=xt_tiles[(j, tt)][:].rearrange("p (c w) n -> p c n w", c=PASSES),
            )

        def quantise_x(j):
            codes = work.tile([P, PASSES * XHALF], U32, tag="codes", bufs=5, align_bytes=64)
            scales = work.tile([P, PASSES * XHALF], U8, tag="scales", bufs=5, align_bytes=64)
            nc.vector.quantize_mx(out=codes[:].bitcast(FP8X4), scales=scales[:], in_=grouped_tiles[j][:])
            mx_tiles[j] = (codes, scales)

        def project(m, half):
            g, qk, stream = place(m)
            codes, scales = mx_tiles[2 * g + half]
            if half == 0:
                yt = psum.tile([P, 2, XHALF], F32, tag="yt", bufs=2)
                yt_tiles[m] = yt
            for c in range(PASSES):
                w_cols = slice((2 * qk + c) * P, (2 * qk + c + 1) * P)
                x_cols = slice(c * XHALF, (c + 1) * XHALF)
                nc.tensor.matmul_mx(
                    out=yt_tiles[m][:, half, :],
                    lhsT=w_codes[stream][:, w_cols].bitcast(FP8X4),
                    lhsT_scale=w_scales[stream][:, w_cols],
                    rhs=codes[:, x_cols].bitcast(FP8X4),
                    rhs_scale=scales[:, x_cols],
                    start=(c == 0),
                    stop=(c == PASSES - 1),
                )

        def add_bias(m):
            _, qk, stream = place(m)
            col = 2 * stream + qk
            ybt = work.tile([P, T, P], F32, tag="ybt", bufs=3)
            nc.scalar.activation(
                out=ybt[:].rearrange("p t n -> p (t n)"),
                in_=yt_tiles[m][:].rearrange("p h n -> p (h n)"),
                func=ACT.Identity,
                bias=bias_col[:, col : col + 1],
            )
            ybt_tiles[m] = ybt

        def transpose_back(m, half):
            if half == 0:
                ybp = psum.tile([P, T, D], F32, tag="ybp", bufs=3)
                ybp_tiles[m] = ybp
            ybp = ybp_tiles[m]
            for t in range(half * XT, (half + 1) * XT):
                tokens = ybt_tiles[m][:, t, :]
                if t % 2 == 0:
                    nc.tensor.matmul(out=ybp[:, t, :], lhsT=tokens, rhs=ident[:], start=True, stop=True)
                else:
                    nc.tensor.transpose(ybp[:, t, :], tokens, ident[:])

        def norms(m):
            ss = work.tile([P, T], F32, tag="ss", bufs=3)
            for t in range(T):
                squares = work.tile([P, D], F32, tag="squares", bufs=2)
                nc.scalar.activation(
                    out=squares[:], in_=ybp_tiles[m][:, t, :], func=ACT.Square, accum_out=ss[:, t : t + 1]
                )
            r = work.tile([P, T], F32, tag="r", bufs=3)
            nc.scalar.activation(out=r[:], in_=ss[:], func=ACT.Abs_reciprocal_sqrt, scale=1.0 / D, bias=EPS)
            r_tiles[m] = r

        def rotate(m, pieces):
            g, qk, _ = place(m)
            if m not in parts_tiles:
                parts = work.tile([P, 2, T, D], F32, tag="parts", bufs=4)
                parts_tiles[m] = parts
            for t, s in pieces:
                nc.vector.scalar_tensor_tensor(
                    out=parts_tiles[m][:, s, t, :].rearrange("p (i h) -> p i h", h=2),
                    in0=ybp_tiles[m][:, t, :].rearrange("p (i s) -> p i s", s=2)[:, :, s : s + 1].to_broadcast([P, HALF, 2]),
                    scalar=r_tiles[m][:, t : t + 1],
                    in1=tables[(g // BATCH, qk)][:, t, s, :, :].rearrange("p h i -> p i h"),
                    op0=ALU.mult,
                    op1=ALU.mult,
                )

        def add_and_store(m):
            g, qk, _ = place(m)
            block, b = divmod(g, BATCH)
            parts = parts_tiles[m]
            result = work.tile([P, T, D], F32, tag="result", bufs=4)
            nc.gpsimd.tensor_tensor(out=result[:], in0=parts[:, 0, :, :], in1=parts[:, 1, :, :], op=ALU.add)
            nc.sync.dma_start(
                out=outs[qk][b, block * BLOCK : (block + 1) * BLOCK, 0, :].rearrange("(p t) d -> p t d", t=T),
                in_=result[:],
            )

        pieces = [(t, s) for t in range(T) for s in range(2)]
        pending_tables = []
        with tc.manual_schedule():
            for j in range(STEPS + 7):
                if j % 2 == 0 and j // 2 + LOOKAHEAD < GROUPS:
                    fetch(load_x(j // 2 + LOOKAHEAD))
                if j == 0:
                    quantise_weights(0)
                if 0 <= j - 3 < STEPS:
                    add_bias(j - 3)
                if 0 <= j - 1 < STEPS:
                    quantise_x(j - 1)
                if 0 <= j - 6 < STEPS:
                    rotate(j - 6, pieces[-1:])
                    add_and_store(j - 6)
                if 0 <= j - 5 < STEPS:
                    rotate(j - 5, pieces[:-2])
                for half in range(2):
                    if j < STEPS:
                        transpose_x(j, half)
                    if 0 <= j - 4 < STEPS:
                        transpose_back(j - 4, half)
                if j < STEPS:
                    copy_x(j, 0, nc.scalar.copy)
                    copy_x(j, 1, nc.scalar.copy if j % 2 else nc.vector.tensor_copy)
                if 0 <= j - 5 < STEPS:
                    rotate(j - 5, pieces[-2:-1])
                if j == 1:
                    spread_vectors()
                    for block in range(BLOCKS):
                        for qk in range(2):
                            pending_tables.extend(table_steps(block, qk))
                    for step in pending_tables[:TABLES_AHEAD]:
                        build_table(step)
                    pending_tables = pending_tables[TABLES_AHEAD:]
                if j == 5:
                    quantise_weights(1)
                if j >= 6 and pending_tables:
                    build_table(pending_tables.pop(0))
                if 0 <= j - 2 < STEPS:
                    for half in range(2):
                        project(j - 2, half)
                if 0 <= j - 4 < STEPS:
                    norms(j - 4)
